import numpy as np
import ml_dtypes


def mxq(x, axis, fmt="e4m3"):
    dtype, down = {"e4m3": (ml_dtypes.float8_e4m3fn, 7), "e5m2": (ml_dtypes.float8_e5m2, 14)}[fmt]
    v = np.moveaxis(np.asarray(x, np.float32).astype(ml_dtypes.bfloat16).astype(np.float64), axis, -1)
    blocks = v.reshape(v.shape[:-1] + (-1, 32))
    amax = np.abs(blocks).max(-1, keepdims=True)
    byte = np.maximum(np.where(amax > 0, np.frexp(amax)[1] - 1 + 127, 0) - down, 1)
    scale = np.exp2(byte - 127.0)
    codes = (blocks / scale).astype(np.float32).astype(dtype).astype(np.float64)
    return np.moveaxis((codes * scale).reshape(v.shape), -1, axis)


WIDE = False


def mx_kscale(k):
    if not WIDE:
        return np.ones(k)
    levels = np.array([10, -10, 5, -5, 0])
    if k % 512:
        return np.exp2(np.random.permutation(np.resize(levels, k // 32))).repeat(32)
    a = np.empty((k // 512, 16))
    for p in range(k // 512):
        a[p, :8] = np.random.permutation(np.resize(levels, 8))
        for g in range(8):
            far = levels[np.abs(levels - a[p, g]) >= 10]
            a[p, g + 8] = far[np.random.randint(len(far))]
    return np.exp2(a.ravel()).repeat(32)


BF16 = ml_dtypes.bfloat16


def bf(x):
    return np.asarray(x, np.float32).astype(BF16)


def f64(x):
    return np.asarray(x).astype(np.float64)


B, C, H, D, N, CO = 4, 128, 2048, 512, 4, 512
NC = N * C
EPS = 1e-5


def bn(v, gamma, beta, axes):
    mean = v.mean(axis=axes, keepdims=True)
    var = v.var(axis=axes, keepdims=True)
    return (v - mean) / np.sqrt(var + EPS) * gamma + beta


def setup_inputs():
    u = mx_kscale(NC)
    head = np.maximum(np.random.standard_normal((N, B, C, D)), 0.0) + 0.25 * np.random.standard_normal((N, B, C, D))
    return {'head_res': bf(head * u.reshape(N, 1, C, 1)),
            'W_merge': bf(np.random.standard_normal((CO, NC)) / np.sqrt(NC) / u[None, :]),
            'g_m': bf(1.0 + 0.1 * np.random.standard_normal(CO)),
            'b_m': bf(0.1 * np.random.standard_normal(CO))}


def reference(head_res, W_merge, g_m, b_m):
    cat = f64(head_res).transpose(1, 0, 2, 3).reshape(B, NC, D)
    m = mxq(f64(W_merge), 1, 'e4m3')[None] @ mxq(cat, 1, 'e4m3')
    m = bn(m, f64(g_m)[None, :, None], f64(b_m)[None, :, None], (0, 2))
    return np.maximum(m, 0.0)

@@ -1,0 +1,240 @@
+from contextlib import ExitStack
+
+import concourse.mybir as mybir
+from concourse.masks import make_identity
+
+FLOPS = 2 * 512 * 512 * 2048
+
+F32 = mybir.dt.float32
+BF16 = mybir.dt.bfloat16
+U32 = mybir.dt.uint32
+U8 = mybir.dt.uint8
+FP8X4 = mybir.dt.float8_e4m3fn_x4
+ACT = mybir.ActivationFunctionType
+ALU = mybir.AluOpType
+
+P = 128
+HEADS = 4
+HEAD_PARTS = P // HEADS
+PACK = 4
+SAMPLES = 4
+D = 512
+BLOCKS = 4
+EPS = 1e-5
+BN_STATS_DIM = 6
+V_COLS = (352, 288, 224, 256)
+
+
+def tile_block_height_reducing_filtering_pb_kernel(tc, head_res, W_merge, g_m, b_m, out):
+    nc = tc.nc
+    with ExitStack() as ctx:
+        keep = ctx.enter_context(tc.tile_pool(name="keep", bufs=1))
+        psum = ctx.enter_context(tc.psum_pool(name="psum", bufs=1))
+        ctx.enter_context(tc.manual_schedule())
+
+        w_sb = keep.tile([P, BLOCKS, P, PACK], BF16, name="w_sb")
+        raw = [keep.tile([P, PACK, D], BF16, name="raw%d" % b) for b in range(SAMPLES)]
+        grouped = [keep.tile([P, D, PACK], BF16, name="grouped%d" % b, align_bytes=64) for b in range(SAMPLES)]
+        w_grouped = keep.tile([P, BLOCKS, P, PACK], BF16, name="w_grouped", align_bytes=64)
+        w_codes = keep.tile([P, BLOCKS, P], U32, name="w_codes", align_bytes=64)
+        w_scales = keep.tile([P, BLOCKS, P], U8, name="w_scales", align_bytes=64)
+        c_codes = keep.tile([P, SAMPLES, D], U32, name="c_codes", align_bytes=64)
+        c_scales = keep.tile([P, SAMPLES, D], U8, name="c_scales", align_bytes=64)
+        gain = keep.tile([P, BLOCKS], BF16, name="gain")
+        bias = keep.tile([P, BLOCKS], BF16, name="bias")
+        ident = keep.tile([P, P], BF16, name="ident")
+        eps = keep.tile([P, 1], F32, name="eps")
+        warm = keep.tile([P, 1], F32, name="warm")
+        stats = [keep.tile([P, SAMPLES, BN_STATS_DIM], F32, name="stats%d" % j) for j in range(BLOCKS)]
+        mean_var = [keep.tile([P, 2], F32, name="mean_var%d" % j) for j in range(BLOCKS)]
+        neg_gain_mean = [keep.tile([P, 1], F32, name="neg_gain_mean%d" % j) for j in range(BLOCKS)]
+        inv_std = [keep.tile([P, 1], F32, name="inv_std%d" % j) for j in range(BLOCKS)]
+        scale = [keep.tile([P, 1], F32, name="scale%d" % j) for j in range(BLOCKS)]
+        shift = [keep.tile([P, 1], F32, name="shift%d" % j) for j in range(BLOCKS)]
+        result = [keep.tile([P, SAMPLES, D], F32, name="result%d" % j) for j in range(BLOCKS)]
+        w_t = {}
+        acc = {}
+        w_view = W_merge.rearrange("(p j) (m t) -> p j m t", j=BLOCKS, t=PACK)
+        out_view = out.rearrange("b (p j) d -> j p b d", j=BLOCKS)
+
+        def load_w(j0, j1):
+            nc.sync.dma_start(out=w_sb[:, j0:j1, :, :], in_=w_view[:, j0:j1, :, :])
+
+        def load_sample(b):
+            for n in range(HEADS):
+                nc.sync.dma_start(
+                    out=raw[b][n * HEAD_PARTS:(n + 1) * HEAD_PARTS, :, :],
+                    in_=head_res[n, b].rearrange("(q t) d -> q t d", t=PACK),
+                )
+
+        def transpose_w(j):
+            w_t[j] = psum.tile([P, PACK, P], BF16, name="w_t%d" % j, tag="bank%d" % (SAMPLES + j))
+            for t in range(PACK):
+                nc.tensor.transpose(w_t[j][:, t, :], w_sb[:, j, :, t], ident[:])
+
+        def copy_out_w(j):
+            nc.scalar.copy(out=w_grouped[:, j, :, :], in_=w_t[j][:].rearrange("p t o -> p o t"))
+
+        def quantise_w(j0, j1):
+            nc.vector.quantize_mx(
+                out=w_codes[:, j0:j1, :].rearrange("p j o -> p (j o)").bitcast(FP8X4),
+                scales=w_scales[:, j0:j1, :].rearrange("p j o -> p (j o)"),
+                in_=w_grouped[:, j0:j1, :, :].rearrange("p j o t -> p (j o t)"),
+            )
+
+        def regroup(copy, b, d0, d1):
+            copy(
+                out=grouped[b][:, d0:d1, :].rearrange("p (c i) t -> p c t i", i=4),
+                in_=raw[b][:, :, d0:d1].rearrange("p t (c i) -> p c t i", i=4),
+            )
+
+        def quantise(b):
+            nc.vector.quantize_mx(
+                out=c_codes[:, b, :].bitcast(FP8X4),
+                scales=c_scales[:, b, :],
+                in_=grouped[b][:].rearrange("p d t -> p (d t)"),
+            )
+
+        def mx_pass(j, b):
+            acc[(j, b)] = psum.tile([P, D], F32, name="acc%d_%d" % (j, b), tag="bank%d" % (SAMPLES * (j % 2) + b))
+            nc.tensor.matmul_mx(
+                out=acc[(j, b)][:],
+                lhsT=w_codes[:, j, :].bitcast(FP8X4),
+                lhsT_scale=w_scales[:, j, :],
+                rhs=c_codes[:, b, :].bitcast(FP8X4),
+                rhs_scale=c_scales[:, b, :],
+                start=True,
+                stop=True,
+            )
+
+        def statistics(j, b):
+            nc.vector.bn_stats(out=stats[j][:, b, :], in_=acc[(j, b)][:])
+
+        def aggregate(j):
+            nc.vector.bn_aggr(out=mean_var[j][:], in_=stats[j][:].rearrange("p b s -> p (b s)"))
+            nc.vector.scalar_tensor_tensor(
+                out=neg_gain_mean[j][:], in0=mean_var[j][:, 0:1], scalar=-1.0, in1=gain[:, j:j + 1],
+                op0=ALU.mult, op1=ALU.mult,
+            )
+
+        def inverse_std(j):
+            nc.scalar.activation(
+                out=inv_std[j][:], in_=mean_var[j][:, 1:2], func=ACT.Abs_reciprocal_sqrt, bias=eps[:, 0:1]
+            )
+
+        def scale_shift_on_scalar(j):
+            nc.scalar.activation(out=scale[j][:], in_=gain[:, j:j + 1], func=ACT.Copy, scale=inv_std[j][:, 0:1])
+            nc.scalar.activation(
+                out=shift[j][:], in_=neg_gain_mean[j][:], func=ACT.Identity,
+                scale=inv_std[j][:, 0:1], bias=bias[:, j:j + 1],
+            )
+
+        def scale_shift_on_vector(j):
+            nc.vector.tensor_mul(out=scale[j][:], in0=gain[:, j:j + 1], in1=inv_std[j][:])
+            nc.vector.scalar_tensor_tensor(
+                out=shift[j][:], in0=neg_gain_mean[j][:], scalar=inv_std[j][:, 0:1], in1=bias[:, j:j + 1],
+                op0=ALU.mult, op1=ALU.add,
+            )
+
+        def apply_on_scalar(j, b):
+            nc.scalar.activation(
+                out=result[j][:, b, :], in_=acc[(j, b)][:], func=ACT.Relu,
+                scale=scale[j][:, 0:1], bias=shift[j][:, 0:1],
+            )
+
+        def apply_on_vector(j, b):
+            nc.vector.tensor_scalar(
+                out=result[j][:, b, :], in0=acc[(j, b)][:], scalar1=scale[j][:, 0:1], scalar2=shift[j][:, 0:1],
+                op0=ALU.mult, op1=ALU.add,
+            )
+            nc.vector.tensor_scalar_max(out=result[j][:, b, :], in0=result[j][:, b, :], scalar1=0.0)
+
+        def store(j, b):
+            nc.sync.dma_start(out=out_view[j][:, b, :], in_=result[j][:, b, :])
+
+        load_w(0, 2)
+        for b in range(SAMPLES):
+            load_sample(b)
+        load_w(2, 4)
+        make_identity(nc, ident[:])
+        nc.vector.memset(eps[:], EPS)
+        nc.scalar.activation(out=warm[:], in_=eps[:], func=ACT.Abs_reciprocal_sqrt)
+
+        transpose_w(0)
+        transpose_w(1)
+        copy_out_w(0)
+        regroup(nc.scalar.copy, 0, V_COLS[0], D)
+        copy_out_w(1)
+        nc.scalar.dma_start(out=gain[:], in_=g_m.rearrange("(p j) -> p j", j=BLOCKS))
+        nc.scalar.dma_start(out=bias[:], in_=b_m.rearrange("(p j) -> p j", j=BLOCKS))
+        regroup(nc.vector.tensor_copy, 0, 0, V_COLS[0])
+        quantise(0)
+        quantise_w(0, 2)
+        mx_pass(0, 0)
+        mx_pass(1, 0)
+        regroup(nc.scalar.copy, 1, V_COLS[1], D)
+        regroup(nc.vector.tensor_copy, 1, 0, V_COLS[1])
+        quantise(1)
+        statistics(0, 0)
+        mx_pass(0, 1)
+        mx_pass(1, 1)
+        transpose_w(2)
+        transpose_w(3)
+        for b in (2, 3):
+            regroup(nc.scalar.copy, b, V_COLS[b], D)
+        for b in (2, 3):
+            regroup(nc.vector.tensor_copy, b, 0, V_COLS[b])
+        quantise(2)
+        quantise(3)
+        mx_pass(0, 2)
+        mx_pass(0, 3)
+        for b in (1, 2, 3):
+            statistics(0, b)
+        aggregate(0)
+        copy_out_w(2)
+        copy_out_w(3)
+        quantise_w(2, 4)
+        mx_pass(1, 2)
+        mx_pass(1, 3)
+
+        inverse_std(0)
+        scale_shift_on_scalar(0)
+        for b in range(SAMPLES):
+            apply_on_scalar(0, b)
+            store(0, b)
+            mx_pass(2, b)
+        for b in range(SAMPLES):
+            statistics(1, b)
+        aggregate(1)
+        inverse_std(1)
+        scale_shift_on_scalar(1)
+        for b in range(SAMPLES - 1):
+            apply_on_scalar(1, b)
+            store(1, b)
+            mx_pass(3, b)
+        for b in range(SAMPLES):
+            statistics(2, b)
+        aggregate(2)
+        inverse_std(2)
+        apply_on_scalar(1, 3)
+        store(1, 3)
+        mx_pass(3, 3)
+        statistics(3, 0)
+        scale_shift_on_vector(2)
+        for b in range(SAMPLES - 1):
+            apply_on_scalar(2, b)
+            store(2, b)
+        for b in (1, 2, 3):
+            statistics(3, b)
+        aggregate(3)
+        inverse_std(3)
+        apply_on_scalar(2, 3)
+        store(2, 3)
+        scale_shift_on_vector(3)
+        apply_on_vector(3, 3)
+        for b in (0, 1):
+            apply_on_scalar(3, b)
+            store(3, b)
+        store(3, 3)
+        apply_on_scalar(3, 2)
+        store(3, 2)

@@ -62,7 +62,8 @@ def tile_block_height_reducing_filtering_pb_kernel(tc, head_res, W_merge, g_m, b
 
         def load_sample(b):
             for n in range(HEADS):
-                nc.sync.dma_start(
+                queue = nc.sync if n < HEADS // 2 else nc.scalar
+                queue.dma_start(
                     out=raw[b][n * HEAD_PARTS:(n + 1) * HEAD_PARTS, :, :],
                     in_=head_res[n, b].rearrange("(q t) d -> q t d", t=PACK),
                 )

@@ -33,7 +33,7 @@ def tile_block_height_reducing_filtering_pb_kernel(tc, head_res, W_merge, g_m, b
         ctx.enter_context(tc.manual_schedule())
 
         w_sb = keep.tile([P, BLOCKS, P, PACK], BF16, name="w_sb")
-        raw = [keep.tile([P, PACK, D], BF16, name="raw%d" % b) for b in range(SAMPLES)]
+        raw = keep.tile([P, SAMPLES, PACK, D], BF16, name="raw")
         grouped = [keep.tile([P, D, PACK], BF16, name="grouped%d" % b, align_bytes=64) for b in range(SAMPLES)]
         w_grouped = keep.tile([P, BLOCKS, P, PACK], BF16, name="w_grouped", align_bytes=64)
         w_codes = keep.tile([P, BLOCKS, P], U32, name="w_codes", align_bytes=64)
@@ -58,14 +58,14 @@ def tile_block_height_reducing_filtering_pb_kernel(tc, head_res, W_merge, g_m, b
         out_view = out.rearrange("b (p j) d -> j p b d", j=BLOCKS)
 
         def load_w(j0, j1):
-            nc.sync.dma_start(out=w_sb[:, j0:j1, :, :], in_=w_view[:, j0:j1, :, :])
+            nc.gpsimd.dma_start(out=w_sb[:, j0:j1, :, :], in_=w_view[:, j0:j1, :, :])
 
-        def load_sample(b):
+        def load_samples(b0, b1):
             for n in range(HEADS):
                 queue = nc.sync if n < HEADS // 2 else nc.scalar
                 queue.dma_start(
-                    out=raw[b][n * HEAD_PARTS:(n + 1) * HEAD_PARTS, :, :],
-                    in_=head_res[n, b].rearrange("(q t) d -> q t d", t=PACK),
+                    out=raw[n * HEAD_PARTS:(n + 1) * HEAD_PARTS, b0:b1, :, :].rearrange("q b t d -> q b (t d)"),
+                    in_=head_res[n, b0:b1].rearrange("b (q t) d -> q b (t d)", t=PACK),
                 )
 
         def transpose_w(j):
@@ -86,7 +86,7 @@ def tile_block_height_reducing_filtering_pb_kernel(tc, head_res, W_merge, g_m, b
         def regroup(copy, b, d0, d1):
             copy(
                 out=grouped[b][:, d0:d1, :].rearrange("p (c i) t -> p c t i", i=4),
-                in_=raw[b][:, :, d0:d1].rearrange("p t (c i) -> p c t i", i=4),
+                in_=raw[:, b, :, d0:d1].rearrange("p t (c i) -> p c t i", i=4),
             )
 
         def quantise(b):
@@ -154,20 +154,21 @@ def tile_block_height_reducing_filtering_pb_kernel(tc, head_res, W_merge, g_m, b
             nc.sync.dma_start(out=out_view[j][:, b, :], in_=result[j][:, b, :])
 
         load_w(0, 2)
-        for b in range(SAMPLES):
-            load_sample(b)
-        load_w(2, 4)
+        load_samples(0, 1)
+        load_samples(1, 2)
         make_identity(nc, ident[:])
+        load_w(2, 4)
+        nc.gpsimd.dma_start(out=gain[:], in_=g_m.rearrange("(p j) -> p j", j=BLOCKS))
+        nc.gpsimd.dma_start(out=bias[:], in_=b_m.rearrange("(p j) -> p j", j=BLOCKS))
         nc.vector.memset(eps[:], EPS)
         nc.scalar.activation(out=warm[:], in_=eps[:], func=ACT.Abs_reciprocal_sqrt)
+        load_samples(2, 4)
 
         transpose_w(0)
         transpose_w(1)
         copy_out_w(0)
         regroup(nc.scalar.copy, 0, V_COLS[0], D)
         copy_out_w(1)
-        nc.scalar.dma_start(out=gain[:], in_=g_m.rearrange("(p j) -> p j", j=BLOCKS))
-        nc.scalar.dma_start(out=bias[:], in_=b_m.rearrange("(p j) -> p j", j=BLOCKS))
         regroup(nc.vector.tensor_copy, 0, 0, V_COLS[0])
         quantise(0)
         quantise_w(0, 2)

@@ -22,7 +22,7 @@ D = 512
 BLOCKS = 4
 EPS = 1e-5
 BN_STATS_DIM = 6
-V_COLS = (352, 288, 224, 256)
+V_COLS = (432, 256, 288, 144)
 
 
 def tile_block_height_reducing_filtering_pb_kernel(tc, head_res, W_merge, g_m, b_m, out):
@@ -42,7 +42,8 @@ def tile_block_height_reducing_filtering_pb_kernel(tc, head_res, W_merge, g_m, b
         c_scales = keep.tile([P, SAMPLES, D], U8, name="c_scales", align_bytes=64)
         gain = keep.tile([P, BLOCKS], BF16, name="gain")
         bias = keep.tile([P, BLOCKS], BF16, name="bias")
-        ident = keep.tile([P, P], BF16, name="ident")
+        neg_gain = keep.tile([P, BLOCKS], F32, name="neg_gain")
+        ident = keep.tile([P, P], F32, name="ident")
         eps = keep.tile([P, 1], F32, name="eps")
         warm = keep.tile([P, 1], F32, name="warm")
         stats = [keep.tile([P, SAMPLES, BN_STATS_DIM], F32, name="stats%d" % j) for j in range(BLOCKS)]
@@ -58,23 +59,24 @@ def tile_block_height_reducing_filtering_pb_kernel(tc, head_res, W_merge, g_m, b
         out_view = out.rearrange("b (p j) d -> j p b d", j=BLOCKS)
 
         def load_w(j0, j1):
-            nc.gpsimd.dma_start(out=w_sb[:, j0:j1, :, :], in_=w_view[:, j0:j1, :, :])
+            nc.sync.dma_start(out=w_sb[:, j0:j1, :, :], in_=w_view[:, j0:j1, :, :])
 
-        def load_samples(b0, b1):
-            for n in range(HEADS):
-                queue = nc.sync if n < HEADS // 2 else nc.scalar
-                queue.dma_start(
-                    out=raw[n * HEAD_PARTS:(n + 1) * HEAD_PARTS, b0:b1, :, :].rearrange("q b t d -> q b (t d)"),
-                    in_=head_res[n, b0:b1].rearrange("b (q t) d -> q b (t d)", t=PACK),
-                )
+        def load_head(queue, n, b):
+            queue.dma_start(
+                out=raw[n * HEAD_PARTS:(n + 1) * HEAD_PARTS, b, :, :],
+                in_=head_res[n, b].rearrange("(q t) d -> q t d", t=PACK),
+            )
 
-        def transpose_w(j):
-            w_t[j] = psum.tile([P, PACK, P], BF16, name="w_t%d" % j, tag="bank%d" % (SAMPLES + j))
-            for t in range(PACK):
-                nc.tensor.transpose(w_t[j][:, t, :], w_sb[:, j, :, t], ident[:])
+        def transpose_w(j0):
+            w_t[j0] = psum.tile([P, 2, 2, P], F32, name="w_t%d" % j0, tag="bank%d" % (SAMPLES + j0))
+            for j in (0, 1):
+                for u in (0, 1):
+                    nc.tensor.transpose(w_t[j0][:, j, u, :], w_sb[:, j0 + j, :, :].bitcast(F32)[:, :, u], ident[:])
 
-        def copy_out_w(j):
-            nc.scalar.copy(out=w_grouped[:, j, :, :], in_=w_t[j][:].rearrange("p t o -> p o t"))
+        def copy_out_w(j0):
+            nc.scalar.copy(
+                out=w_grouped[:, j0:j0 + 2, :, :].bitcast(F32), in_=w_t[j0][:].rearrange("m j u o -> m j o u")
+            )
 
         def quantise_w(j0, j1):
             nc.vector.quantize_mx(
@@ -113,10 +115,7 @@ def tile_block_height_reducing_filtering_pb_kernel(tc, head_res, W_merge, g_m, b
 
         def aggregate(j):
             nc.vector.bn_aggr(out=mean_var[j][:], in_=stats[j][:].rearrange("p b s -> p (b s)"))
-            nc.vector.scalar_tensor_tensor(
-                out=neg_gain_mean[j][:], in0=mean_var[j][:, 0:1], scalar=-1.0, in1=gain[:, j:j + 1],
-                op0=ALU.mult, op1=ALU.mult,
-            )
+            nc.gpsimd.tensor_mul(out=neg_gain_mean[j][:], in0=mean_var[j][:, 0:1], in1=neg_gain[:, j:j + 1])
 
         def inverse_std(j):
             nc.scalar.activation(
@@ -143,97 +142,96 @@ def tile_block_height_reducing_filtering_pb_kernel(tc, head_res, W_merge, g_m, b
                 scale=scale[j][:, 0:1], bias=shift[j][:, 0:1],
             )
 
-        def apply_on_vector(j, b):
+        def affine_on_vector(j, b):
             nc.vector.tensor_scalar(
                 out=result[j][:, b, :], in0=acc[(j, b)][:], scalar1=scale[j][:, 0:1], scalar2=shift[j][:, 0:1],
                 op0=ALU.mult, op1=ALU.add,
             )
+
+        def relu_on_vector(j, b):
             nc.vector.tensor_scalar_max(out=result[j][:, b, :], in0=result[j][:, b, :], scalar1=0.0)
 
         def store(j, b):
             nc.sync.dma_start(out=out_view[j][:, b, :], in_=result[j][:, b, :])
 
+        for n, queue in ((0, nc.sync), (2, nc.scalar), (1, nc.sync), (3, nc.scalar)):
+            load_head(queue, n, 0)
         load_w(0, 2)
-        load_samples(0, 1)
-        load_samples(1, 2)
-        make_identity(nc, ident[:])
-        load_w(2, 4)
-        nc.gpsimd.dma_start(out=gain[:], in_=g_m.rearrange("(p j) -> p j", j=BLOCKS))
-        nc.gpsimd.dma_start(out=bias[:], in_=b_m.rearrange("(p j) -> p j", j=BLOCKS))
+        for n, queue in ((0, nc.sync), (2, nc.scalar), (1, nc.gpsimd), (3, nc.scalar)):
+            load_head(queue, n, 1)
         nc.vector.memset(eps[:], EPS)
         nc.scalar.activation(out=warm[:], in_=eps[:], func=ACT.Abs_reciprocal_sqrt)
-        load_samples(2, 4)
+        make_identity(nc, ident[:])
+        for n, queue in ((0, nc.sync), (2, nc.scalar), (1, nc.sync), (3, nc.scalar)):
+            load_head(queue, n, 2)
+        load_w(2, 4)
+        for n, queue in ((0, nc.sync), (2, nc.gpsimd), (1, nc.sync), (3, nc.gpsimd)):
+            load_head(queue, n, 3)
+        nc.sync.dma_start(out=gain[:], in_=g_m.rearrange("(p j) -> p j", j=BLOCKS))
+        nc.sync.dma_start(out=bias[:], in_=b_m.rearrange("(p j) -> p j", j=BLOCKS))
+        nc.gpsimd.tensor_scalar(out=neg_gain[:], in0=gain[:], scalar1=-1.0, scalar2=0.0, op0=ALU.mult, op1=ALU.add)
 
         transpose_w(0)
-        transpose_w(1)
-        copy_out_w(0)
         regroup(nc.scalar.copy, 0, V_COLS[0], D)
-        copy_out_w(1)
-        regroup(nc.vector.tensor_copy, 0, 0, V_COLS[0])
+        regroup(nc.scalar.copy, 1, V_COLS[1], D)
+        copy_out_w(0)
+        regroup(nc.scalar.copy, 2, V_COLS[2], D)
+        for b in (0, 1):
+            regroup(nc.vector.tensor_copy, b, 0, V_COLS[b])
         quantise(0)
+        quantise(1)
+        regroup(nc.vector.tensor_copy, 2, 0, V_COLS[2])
         quantise_w(0, 2)
         mx_pass(0, 0)
-        mx_pass(1, 0)
-        regroup(nc.scalar.copy, 1, V_COLS[1], D)
-        regroup(nc.vector.tensor_copy, 1, 0, V_COLS[1])
-        quantise(1)
-        statistics(0, 0)
         mx_pass(0, 1)
-        mx_pass(1, 1)
-        transpose_w(2)
-        transpose_w(3)
-        for b in (2, 3):
-            regroup(nc.scalar.copy, b, V_COLS[b], D)
-        for b in (2, 3):
-            regroup(nc.vector.tensor_copy, b, 0, V_COLS[b])
         quantise(2)
-        quantise(3)
         mx_pass(0, 2)
+        transpose_w(2)
+        mx_pass(1, 0)
+        regroup(nc.scalar.copy, 3, V_COLS[3], D)
+        copy_out_w(2)
+        regroup(nc.vector.tensor_copy, 3, 0, V_COLS[3])
+        statistics(0, 0)
+        quantise(3)
         mx_pass(0, 3)
         for b in (1, 2, 3):
+            mx_pass(1, b)
+        for b in (1, 2, 3):
             statistics(0, b)
+        quantise_w(2, 3)
         aggregate(0)
-        copy_out_w(2)
-        copy_out_w(3)
-        quantise_w(2, 4)
-        mx_pass(1, 2)
-        mx_pass(1, 3)
-
         inverse_std(0)
         scale_shift_on_scalar(0)
-        for b in range(SAMPLES):
-            apply_on_scalar(0, b)
-            store(0, b)
-            mx_pass(2, b)
+
         for b in range(SAMPLES):
             statistics(1, b)
+        quantise_w(3, 4)
         aggregate(1)
-        inverse_std(1)
-        scale_shift_on_scalar(1)
-        for b in range(SAMPLES - 1):
-            apply_on_scalar(1, b)
-            store(1, b)
-            mx_pass(3, b)
-        for b in range(SAMPLES):
-            statistics(2, b)
-        aggregate(2)
-        inverse_std(2)
-        apply_on_scalar(1, 3)
-        store(1, 3)
-        mx_pass(3, 3)
-        statistics(3, 0)
-        scale_shift_on_vector(2)
+        for j in (0, 1):
+            for b in range(SAMPLES - 1):
+                apply_on_scalar(j, b)
+                store(j, b)
+                mx_pass(j + 2, b)
+            inverse_std(j + 1)
+            apply_on_scalar(j, SAMPLES - 1)
+            store(j, SAMPLES - 1)
+            mx_pass(j + 2, SAMPLES - 1)
+            statistics(j + 2, 0)
+            scale_shift_on_vector(j + 1)
+            for b in range(1, SAMPLES):
+                statistics(j + 2, b)
+            aggregate(j + 2)
+
         for b in range(SAMPLES - 1):
             apply_on_scalar(2, b)
             store(2, b)
-        for b in (1, 2, 3):
-            statistics(3, b)
-        aggregate(3)
         inverse_std(3)
-        apply_on_scalar(2, 3)
-        store(2, 3)
+        affine_on_vector(2, 3)
         scale_shift_on_vector(3)
-        apply_on_vector(3, 3)
+        relu_on_vector(2, 3)
+        store(2, 3)
+        affine_on_vector(3, 3)
+        relu_on_vector(3, 3)
         for b in (0, 1):
             apply_on_scalar(3, b)
             store(3, b)

@@ -42,7 +42,6 @@ def tile_block_height_reducing_filtering_pb_kernel(tc, head_res, W_merge, g_m, b
         c_scales = keep.tile([P, SAMPLES, D], U8, name="c_scales", align_bytes=64)
         gain = keep.tile([P, BLOCKS], BF16, name="gain")
         bias = keep.tile([P, BLOCKS], BF16, name="bias")
-        neg_gain = keep.tile([P, BLOCKS], F32, name="neg_gain")
         ident = keep.tile([P, P], F32, name="ident")
         eps = keep.tile([P, 1], F32, name="eps")
         warm = keep.tile([P, 1], F32, name="warm")
@@ -115,7 +114,12 @@ def tile_block_height_reducing_filtering_pb_kernel(tc, head_res, W_merge, g_m, b
 
         def aggregate(j):
             nc.vector.bn_aggr(out=mean_var[j][:], in_=stats[j][:].rearrange("p b s -> p (b s)"))
-            nc.gpsimd.tensor_mul(out=neg_gain_mean[j][:], in0=mean_var[j][:, 0:1], in1=neg_gain[:, j:j + 1])
+
+        def negate_gain_mean(j):
+            nc.vector.scalar_tensor_tensor(
+                out=neg_gain_mean[j][:], in0=mean_var[j][:, 0:1], scalar=-1.0, in1=gain[:, j:j + 1],
+                op0=ALU.mult, op1=ALU.mult,
+            )
 
         def inverse_std(j):
             nc.scalar.activation(
@@ -157,7 +161,7 @@ def tile_block_height_reducing_filtering_pb_kernel(tc, head_res, W_merge, g_m, b
         for n, queue in ((0, nc.sync), (2, nc.scalar), (1, nc.sync), (3, nc.scalar)):
             load_head(queue, n, 0)
         load_w(0, 2)
-        for n, queue in ((0, nc.sync), (2, nc.scalar), (1, nc.gpsimd), (3, nc.scalar)):
+        for n, queue in ((2, nc.scalar), (0, nc.sync), (3, nc.scalar), (1, nc.sync)):
             load_head(queue, n, 1)
         nc.vector.memset(eps[:], EPS)
         nc.scalar.activation(out=warm[:], in_=eps[:], func=ACT.Abs_reciprocal_sqrt)
@@ -165,11 +169,10 @@ def tile_block_height_reducing_filtering_pb_kernel(tc, head_res, W_merge, g_m, b
         for n, queue in ((0, nc.sync), (2, nc.scalar), (1, nc.sync), (3, nc.scalar)):
             load_head(queue, n, 2)
         load_w(2, 4)
-        for n, queue in ((0, nc.sync), (2, nc.gpsimd), (1, nc.sync), (3, nc.gpsimd)):
-            load_head(queue, n, 3)
+        for n in (0, 2, 1, 3):
+            load_head(nc.sync, n, 3)
         nc.sync.dma_start(out=gain[:], in_=g_m.rearrange("(p j) -> p j", j=BLOCKS))
         nc.sync.dma_start(out=bias[:], in_=b_m.rearrange("(p j) -> p j", j=BLOCKS))
-        nc.gpsimd.tensor_scalar(out=neg_gain[:], in0=gain[:], scalar1=-1.0, scalar2=0.0, op0=ALU.mult, op1=ALU.add)
 
         transpose_w(0)
         regroup(nc.scalar.copy, 0, V_COLS[0], D)
@@ -201,9 +204,11 @@ def tile_block_height_reducing_filtering_pb_kernel(tc, head_res, W_merge, g_m, b
         quantise_w(2, 3)
         aggregate(0)
         inverse_std(0)
+        statistics(1, 0)
+        negate_gain_mean(0)
         scale_shift_on_scalar(0)
 
-        for b in range(SAMPLES):
+        for b in range(1, SAMPLES):
             statistics(1, b)
         quantise_w(3, 4)
         aggregate(1)
@@ -217,6 +222,7 @@ def tile_block_height_reducing_filtering_pb_kernel(tc, head_res, W_merge, g_m, b
             store(j, SAMPLES - 1)
             mx_pass(j + 2, SAMPLES - 1)
             statistics(j + 2, 0)
+            negate_gain_mean(j + 1)
             scale_shift_on_vector(j + 1)
             for b in range(1, SAMPLES):
                 statistics(j + 2, b)
@@ -227,6 +233,7 @@ def tile_block_height_reducing_filtering_pb_kernel(tc, head_res, W_merge, g_m, b
             store(2, b)
         inverse_std(3)
         affine_on_vector(2, 3)
+        negate_gain_mean(3)
         scale_shift_on_vector(3)
         relu_on_vector(2, 3)
         store(2, 3)

@@ -22,7 +22,7 @@ D = 512
 BLOCKS = 4
 EPS = 1e-5
 BN_STATS_DIM = 6
-V_COLS = (432, 256, 288, 144)
+V_COLS = (344, 240, 248, 136)
 
 
 def tile_block_height_reducing_filtering_pb_kernel(tc, head_res, W_merge, g_m, b_m, out):
@@ -52,6 +52,7 @@ def tile_block_height_reducing_filtering_pb_kernel(tc, head_res, W_merge, g_m, b
         scale = [keep.tile([P, 1], F32, name="scale%d" % j) for j in range(BLOCKS)]
         shift = [keep.tile([P, 1], F32, name="shift%d" % j) for j in range(BLOCKS)]
         result = [keep.tile([P, SAMPLES, D], F32, name="result%d" % j) for j in range(BLOCKS)]
+        delay = keep.tile([P, 8 * D], BF16, name="delay")
         w_t = {}
         acc = {}
         w_view = W_merge.rearrange("(p j) (m t) -> p j m t", j=BLOCKS, t=PACK)
@@ -60,11 +61,12 @@ def tile_block_height_reducing_filtering_pb_kernel(tc, head_res, W_merge, g_m, b
         def load_w(j0, j1):
             nc.sync.dma_start(out=w_sb[:, j0:j1, :, :], in_=w_view[:, j0:j1, :, :])
 
-        def load_head(queue, n, b):
-            queue.dma_start(
-                out=raw[n * HEAD_PARTS:(n + 1) * HEAD_PARTS, b, :, :],
-                in_=head_res[n, b].rearrange("(q t) d -> q t d", t=PACK),
-            )
+        def load_sample(b):
+            for n in (0, 2, 1, 3):
+                nc.sync.dma_start(
+                    out=raw[n * HEAD_PARTS:(n + 1) * HEAD_PARTS, b, :, :],
+                    in_=head_res[n, b].rearrange("(q t) d -> q t d", t=PACK),
+                )
 
         def transpose_w(j0):
             w_t[j0] = psum.tile([P, 2, 2, P], F32, name="w_t%d" % j0, tag="bank%d" % (SAMPLES + j0))
@@ -158,19 +160,18 @@ def tile_block_height_reducing_filtering_pb_kernel(tc, head_res, W_merge, g_m, b
         def store(j, b):
             nc.sync.dma_start(out=out_view[j][:, b, :], in_=result[j][:, b, :])
 
-        for n, queue in ((0, nc.sync), (2, nc.scalar), (1, nc.sync), (3, nc.scalar)):
-            load_head(queue, n, 0)
+        nc.sync.dma_start(
+            out=delay[0:HEAD_PARTS:4, :], in_=head_res[0, 0].rearrange("(m c) d -> m (c d)", c=8)[0:8, :]
+        )
+        load_sample(0)
         load_w(0, 2)
-        for n, queue in ((2, nc.scalar), (0, nc.sync), (3, nc.scalar), (1, nc.sync)):
-            load_head(queue, n, 1)
+        load_sample(1)
         nc.vector.memset(eps[:], EPS)
         nc.scalar.activation(out=warm[:], in_=eps[:], func=ACT.Abs_reciprocal_sqrt)
         make_identity(nc, ident[:])
-        for n, queue in ((0, nc.sync), (2, nc.scalar), (1, nc.sync), (3, nc.scalar)):
-            load_head(queue, n, 2)
+        load_sample(2)
         load_w(2, 4)
-        for n in (0, 2, 1, 3):
-            load_head(nc.sync, n, 3)
+        load_sample(3)
         nc.sync.dma_start(out=gain[:], in_=g_m.rearrange("(p j) -> p j", j=BLOCKS))
         nc.sync.dma_start(out=bias[:], in_=b_m.rearrange("(p j) -> p j", j=BLOCKS))
 

@@ -22,7 +22,7 @@ D = 512
 BLOCKS = 4
 EPS = 1e-5
 BN_STATS_DIM = 6
-V_COLS = (344, 240, 248, 136)
+V_COLS = (256, 192, 192, 344)
 
 
 def tile_block_height_reducing_filtering_pb_kernel(tc, head_res, W_merge, g_m, b_m, out):
@@ -52,7 +52,6 @@ def tile_block_height_reducing_filtering_pb_kernel(tc, head_res, W_merge, g_m, b
         scale = [keep.tile([P, 1], F32, name="scale%d" % j) for j in range(BLOCKS)]
         shift = [keep.tile([P, 1], F32, name="shift%d" % j) for j in range(BLOCKS)]
         result = [keep.tile([P, SAMPLES, D], F32, name="result%d" % j) for j in range(BLOCKS)]
-        delay = keep.tile([P, 8 * D], BF16, name="delay")
         w_t = {}
         acc = {}
         w_view = W_merge.rearrange("(p j) (m t) -> p j m t", j=BLOCKS, t=PACK)
@@ -68,8 +67,8 @@ def tile_block_height_reducing_filtering_pb_kernel(tc, head_res, W_merge, g_m, b
                     in_=head_res[n, b].rearrange("(q t) d -> q t d", t=PACK),
                 )
 
-        def transpose_w(j0):
-            w_t[j0] = psum.tile([P, 2, 2, P], F32, name="w_t%d" % j0, tag="bank%d" % (SAMPLES + j0))
+        def transpose_w(j0, b):
+            w_t[j0] = psum.tile([P, 2, 2, P], F32, name="w_t%d" % j0, tag="bank%d" % (SAMPLES + b))
             for j in (0, 1):
                 for u in (0, 1):
                     nc.tensor.transpose(w_t[j0][:, j, u, :], w_sb[:, j0 + j, :, :].bitcast(F32)[:, :, u], ident[:])
@@ -160,89 +159,104 @@ def tile_block_height_reducing_filtering_pb_kernel(tc, head_res, W_merge, g_m, b
         def store(j, b):
             nc.sync.dma_start(out=out_view[j][:, b, :], in_=result[j][:, b, :])
 
-        nc.sync.dma_start(
-            out=delay[0:HEAD_PARTS:4, :], in_=head_res[0, 0].rearrange("(m c) d -> m (c d)", c=8)[0:8, :]
-        )
         load_sample(0)
         load_w(0, 2)
-        load_sample(1)
+        for b in (1, 2, 3):
+            load_sample(b)
+        load_w(2, 4)
+        make_identity(nc, ident[:])
         nc.vector.memset(eps[:], EPS)
         nc.scalar.activation(out=warm[:], in_=eps[:], func=ACT.Abs_reciprocal_sqrt)
-        make_identity(nc, ident[:])
-        load_sample(2)
-        load_w(2, 4)
-        load_sample(3)
         nc.sync.dma_start(out=gain[:], in_=g_m.rearrange("(p j) -> p j", j=BLOCKS))
         nc.sync.dma_start(out=bias[:], in_=b_m.rearrange("(p j) -> p j", j=BLOCKS))
 
-        transpose_w(0)
+        transpose_w(0, 0)
         regroup(nc.scalar.copy, 0, V_COLS[0], D)
-        regroup(nc.scalar.copy, 1, V_COLS[1], D)
         copy_out_w(0)
+        regroup(nc.scalar.copy, 1, V_COLS[1], D)
         regroup(nc.scalar.copy, 2, V_COLS[2], D)
-        for b in (0, 1):
-            regroup(nc.vector.tensor_copy, b, 0, V_COLS[b])
+        regroup(nc.vector.tensor_copy, 0, 0, V_COLS[0])
         quantise(0)
-        quantise(1)
-        regroup(nc.vector.tensor_copy, 2, 0, V_COLS[2])
         quantise_w(0, 2)
         mx_pass(0, 0)
+        mx_pass(1, 0)
+        regroup(nc.vector.tensor_copy, 1, 0, V_COLS[1])
+        statistics(0, 0)
+        quantise(1)
         mx_pass(0, 1)
+        mx_pass(1, 1)
+        statistics(1, 0)
+        regroup(nc.vector.tensor_copy, 2, 0, V_COLS[2])
+        statistics(0, 1)
         quantise(2)
         mx_pass(0, 2)
-        transpose_w(2)
-        mx_pass(1, 0)
+        mx_pass(1, 2)
+        statistics(1, 1)
+        statistics(0, 2)
+        statistics(1, 2)
+
         regroup(nc.scalar.copy, 3, V_COLS[3], D)
-        copy_out_w(2)
         regroup(nc.vector.tensor_copy, 3, 0, V_COLS[3])
-        statistics(0, 0)
         quantise(3)
+        transpose_w(2, 3)
         mx_pass(0, 3)
-        for b in (1, 2, 3):
-            mx_pass(1, b)
-        for b in (1, 2, 3):
-            statistics(0, b)
-        quantise_w(2, 3)
+        copy_out_w(2)
+        mx_pass(1, 3)
+        statistics(0, 3)
         aggregate(0)
         inverse_std(0)
-        statistics(1, 0)
+        statistics(1, 3)
         negate_gain_mean(0)
         scale_shift_on_scalar(0)
-
-        for b in range(1, SAMPLES):
-            statistics(1, b)
-        quantise_w(3, 4)
         aggregate(1)
-        for j in (0, 1):
-            for b in range(SAMPLES - 1):
-                apply_on_scalar(j, b)
-                store(j, b)
-                mx_pass(j + 2, b)
-            inverse_std(j + 1)
-            apply_on_scalar(j, SAMPLES - 1)
-            store(j, SAMPLES - 1)
-            mx_pass(j + 2, SAMPLES - 1)
-            statistics(j + 2, 0)
-            negate_gain_mean(j + 1)
-            scale_shift_on_vector(j + 1)
-            for b in range(1, SAMPLES):
-                statistics(j + 2, b)
-            aggregate(j + 2)
 
-        for b in range(SAMPLES - 1):
+        apply_on_scalar(0, 0)
+        store(0, 0)
+        quantise_w(2, 4)
+        mx_pass(2, 0)
+        inverse_std(1)
+        negate_gain_mean(1)
+        scale_shift_on_vector(1)
+        affine_on_vector(0, 3)
+        apply_on_scalar(0, 1)
+        store(0, 1)
+        mx_pass(2, 1)
+        relu_on_vector(0, 3)
+        store(0, 3)
+        mx_pass(2, 3)
+        apply_on_scalar(0, 2)
+        store(0, 2)
+        mx_pass(2, 2)
+        for b in (0, 1, 3, 2):
+            statistics(2, b)
+        aggregate(2)
+        for b in (0, 1, 2):
+            apply_on_scalar(1, b)
+            store(1, b)
+            mx_pass(3, b)
+        inverse_std(2)
+        apply_on_scalar(1, 3)
+        store(1, 3)
+        mx_pass(3, 3)
+        statistics(3, 0)
+        negate_gain_mean(2)
+        scale_shift_on_vector(2)
+        for b in (1, 2, 3):
+            statistics(3, b)
+        aggregate(3)
+        for b in (0, 1, 2):
             apply_on_scalar(2, b)
             store(2, b)
         inverse_std(3)
-        affine_on_vector(2, 3)
         negate_gain_mean(3)
         scale_shift_on_vector(3)
-        relu_on_vector(2, 3)
+        apply_on_scalar(2, 3)
         store(2, 3)
-        affine_on_vector(3, 3)
-        relu_on_vector(3, 3)
+        for b in (3, 2):
+            affine_on_vector(3, b)
+            relu_on_vector(3, b)
         for b in (0, 1):
             apply_on_scalar(3, b)
             store(3, b)
-        store(3, 3)
-        apply_on_scalar(3, 2)
-        store(3, 2)
+        for b in (3, 2):
+            store(3, b)

@@ -22,7 +22,7 @@ D = 512
 BLOCKS = 4
 EPS = 1e-5
 BN_STATS_DIM = 6
-V_COLS = (256, 192, 192, 344)
+V_COLS = (160, 160, 160, 304)
 
 
 def tile_block_height_reducing_filtering_pb_kernel(tc, head_res, W_merge, g_m, b_m, out):
@@ -91,21 +91,22 @@ def tile_block_height_reducing_filtering_pb_kernel(tc, head_res, W_merge, g_m, b
                 in_=raw[:, b, :, d0:d1].rearrange("p t (c i) -> p c t i", i=4),
             )
 
-        def quantise(b):
+        def quantise(b, d0=0, d1=D):
             nc.vector.quantize_mx(
-                out=c_codes[:, b, :].bitcast(FP8X4),
-                scales=c_scales[:, b, :],
-                in_=grouped[b][:].rearrange("p d t -> p (d t)"),
+                out=c_codes[:, b, d0:d1].bitcast(FP8X4),
+                scales=c_scales[:, b, d0:d1],
+                in_=grouped[b][:, d0:d1, :].rearrange("p d t -> p (d t)"),
             )
 
-        def mx_pass(j, b):
-            acc[(j, b)] = psum.tile([P, D], F32, name="acc%d_%d" % (j, b), tag="bank%d" % (SAMPLES * (j % 2) + b))
+        def mx_pass(j, b, d0=0, d1=D):
+            if d0 == 0:
+                acc[(j, b)] = psum.tile([P, D], F32, name="acc%d_%d" % (j, b), tag="bank%d" % (SAMPLES * (j % 2) + b))
             nc.tensor.matmul_mx(
-                out=acc[(j, b)][:],
+                out=acc[(j, b)][:, d0:d1],
                 lhsT=w_codes[:, j, :].bitcast(FP8X4),
                 lhsT_scale=w_scales[:, j, :],
-                rhs=c_codes[:, b, :].bitcast(FP8X4),
-                rhs_scale=c_scales[:, b, :],
+                rhs=c_codes[:, b, d0:d1].bitcast(FP8X4),
+                rhs_scale=c_scales[:, b, d0:d1],
                 start=True,
                 stop=True,
             )
@@ -159,6 +160,8 @@ def tile_block_height_reducing_filtering_pb_kernel(tc, head_res, W_merge, g_m, b
         def store(j, b):
             nc.sync.dma_start(out=out_view[j][:, b, :], in_=result[j][:, b, :])
 
+        nc.scalar.dma_start(out=gain[:], in_=g_m.rearrange("(p j) -> p j", j=BLOCKS))
+        nc.scalar.dma_start(out=bias[:], in_=b_m.rearrange("(p j) -> p j", j=BLOCKS))
         load_sample(0)
         load_w(0, 2)
         for b in (1, 2, 3):
@@ -167,8 +170,6 @@ def tile_block_height_reducing_filtering_pb_kernel(tc, head_res, W_merge, g_m, b
         make_identity(nc, ident[:])
         nc.vector.memset(eps[:], EPS)
         nc.scalar.activation(out=warm[:], in_=eps[:], func=ACT.Abs_reciprocal_sqrt)
-        nc.sync.dma_start(out=gain[:], in_=g_m.rearrange("(p j) -> p j", j=BLOCKS))
-        nc.sync.dma_start(out=bias[:], in_=b_m.rearrange("(p j) -> p j", j=BLOCKS))
 
         transpose_w(0, 0)
         regroup(nc.scalar.copy, 0, V_COLS[0], D)
@@ -177,86 +178,64 @@ def tile_block_height_reducing_filtering_pb_kernel(tc, head_res, W_merge, g_m, b
         regroup(nc.scalar.copy, 2, V_COLS[2], D)
         regroup(nc.vector.tensor_copy, 0, 0, V_COLS[0])
         quantise(0)
+        regroup(nc.vector.tensor_copy, 1, 0, V_COLS[1])
         quantise_w(0, 2)
         mx_pass(0, 0)
         mx_pass(1, 0)
-        regroup(nc.vector.tensor_copy, 1, 0, V_COLS[1])
-        statistics(0, 0)
         quantise(1)
         mx_pass(0, 1)
         mx_pass(1, 1)
-        statistics(1, 0)
+        statistics(0, 0)
         regroup(nc.vector.tensor_copy, 2, 0, V_COLS[2])
-        statistics(0, 1)
+        statistics(1, 0)
         quantise(2)
         mx_pass(0, 2)
-        mx_pass(1, 2)
-        statistics(1, 1)
-        statistics(0, 2)
-        statistics(1, 2)
+        statistics(0, 1)
 
         regroup(nc.scalar.copy, 3, V_COLS[3], D)
-        regroup(nc.vector.tensor_copy, 3, 0, V_COLS[3])
-        quantise(3)
+        regroup(nc.vector.tensor_copy, 3, 0, D // 2)
+        regroup(nc.vector.tensor_copy, 3, D // 2, V_COLS[3])
         transpose_w(2, 3)
-        mx_pass(0, 3)
+        for d0 in (0, D // 2):
+            quantise(3, d0, d0 + D // 2)
+            mx_pass(0, 3, d0, d0 + D // 2)
         copy_out_w(2)
+        mx_pass(1, 2)
         mx_pass(1, 3)
+        statistics(0, 2)
         statistics(0, 3)
         aggregate(0)
         inverse_std(0)
-        statistics(1, 3)
+        quantise_w(2, 4)
         negate_gain_mean(0)
         scale_shift_on_scalar(0)
+        for b in (1, 2, 3):
+            statistics(1, b)
         aggregate(1)
 
-        apply_on_scalar(0, 0)
-        store(0, 0)
-        quantise_w(2, 4)
-        mx_pass(2, 0)
-        inverse_std(1)
-        negate_gain_mean(1)
-        scale_shift_on_vector(1)
-        affine_on_vector(0, 3)
-        apply_on_scalar(0, 1)
-        store(0, 1)
-        mx_pass(2, 1)
-        relu_on_vector(0, 3)
-        store(0, 3)
-        mx_pass(2, 3)
-        apply_on_scalar(0, 2)
-        store(0, 2)
-        mx_pass(2, 2)
-        for b in (0, 1, 3, 2):
-            statistics(2, b)
-        aggregate(2)
-        for b in (0, 1, 2):
-            apply_on_scalar(1, b)
-            store(1, b)
-            mx_pass(3, b)
-        inverse_std(2)
-        apply_on_scalar(1, 3)
-        store(1, 3)
-        mx_pass(3, 3)
-        statistics(3, 0)
-        negate_gain_mean(2)
-        scale_shift_on_vector(2)
-        for b in (1, 2, 3):
-            statistics(3, b)
-        aggregate(3)
-        for b in (0, 1, 2):
-            apply_on_scalar(2, b)
-            store(2, b)
-        inverse_std(3)
-        negate_gain_mean(3)
-        scale_shift_on_vector(3)
-        apply_on_scalar(2, 3)
-        store(2, 3)
-        for b in (3, 2):
-            affine_on_vector(3, b)
-            relu_on_vector(3, b)
+        for j in range(BLOCKS - 1):
+            for b in range(SAMPLES - 1):
+                apply_on_scalar(j, b)
+                store(j, b)
+                if j + 2 < BLOCKS:
+                    mx_pass(j + 2, b)
+            inverse_std(j + 1)
+            apply_on_scalar(j, SAMPLES - 1)
+            store(j, SAMPLES - 1)
+            if j + 2 < BLOCKS:
+                mx_pass(j + 2, SAMPLES - 1)
+                statistics(j + 2, 0)
+            negate_gain_mean(j + 1)
+            scale_shift_on_vector(j + 1)
+            if j + 2 < BLOCKS:
+                for b in range(1, SAMPLES):
+                    statistics(j + 2, b)
+                aggregate(j + 2)
+        affine_on_vector(3, 3)
+        relu_on_vector(3, 3)
         for b in (0, 1):
             apply_on_scalar(3, b)
             store(3, b)
-        for b in (3, 2):
-            store(3, b)
+        store(3, 3)
+        apply_on_scalar(3, 2)
+        store(3, 2)

from contextlib import ExitStack

import concourse.mybir as mybir
from concourse.masks import make_identity

FLOPS = 2 * 512 * 512 * 2048

F32 = mybir.dt.float32
BF16 = mybir.dt.bfloat16
U32 = mybir.dt.uint32
U8 = mybir.dt.uint8
FP8X4 = mybir.dt.float8_e4m3fn_x4
ACT = mybir.ActivationFunctionType
ALU = mybir.AluOpType

P = 128
HEADS = 4
HEAD_PARTS = P // HEADS
PACK = 4
SAMPLES = 4
D = 512
BLOCKS = 4
EPS = 1e-5
BN_STATS_DIM = 6
V_COLS = (160, 160, 160, 304)


def tile_block_height_reducing_filtering_pb_kernel(tc, head_res, W_merge, g_m, b_m, out):
    nc = tc.nc
    with ExitStack() as ctx:
        keep = ctx.enter_context(tc.tile_pool(name="keep", bufs=1))
        psum = ctx.enter_context(tc.psum_pool(name="psum", bufs=1))
        ctx.enter_context(tc.manual_schedule())

        w_sb = keep.tile([P, BLOCKS, P, PACK], BF16, name="w_sb")
        raw = keep.tile([P, SAMPLES, PACK, D], BF16, name="raw")
        grouped = [keep.tile([P, D, PACK], BF16, name="grouped%d" % b, align_bytes=64) for b in range(SAMPLES)]
        w_grouped = keep.tile([P, BLOCKS, P, PACK], BF16, name="w_grouped", align_bytes=64)
        w_codes = keep.tile([P, BLOCKS, P], U32, name="w_codes", align_bytes=64)
        w_scales = keep.tile([P, BLOCKS, P], U8, name="w_scales", align_bytes=64)
        c_codes = keep.tile([P, SAMPLES, D], U32, name="c_codes", align_bytes=64)
        c_scales = keep.tile([P, SAMPLES, D], U8, name="c_scales", align_bytes=64)
        gain = keep.tile([P, BLOCKS], BF16, name="gain")
        bias = keep.tile([P, BLOCKS], BF16, name="bias")
        ident = keep.tile([P, P], F32, name="ident")
        eps = keep.tile([P, 1], F32, name="eps")
        warm = keep.tile([P, 1], F32, name="warm")
        stats = [keep.tile([P, SAMPLES, BN_STATS_DIM], F32, name="stats%d" % j) for j in range(BLOCKS)]
        mean_var = [keep.tile([P, 2], F32, name="mean_var%d" % j) for j in range(BLOCKS)]
        neg_gain_mean = [keep.tile([P, 1], F32, name="neg_gain_mean%d" % j) for j in range(BLOCKS)]
        inv_std = [keep.tile([P, 1], F32, name="inv_std%d" % j) for j in range(BLOCKS)]
        scale = [keep.tile([P, 1], F32, name="scale%d" % j) for j in range(BLOCKS)]
        shift = [keep.tile([P, 1], F32, name="shift%d" % j) for j in range(BLOCKS)]
        result = [keep.tile([P, SAMPLES, D], F32, name="result%d" % j) for j in range(BLOCKS)]
        w_t = {}
        acc = {}
        w_view = W_merge.rearrange("(p j) (m t) -> p j m t", j=BLOCKS, t=PACK)
        out_view = out.rearrange("b (p j) d -> j p b d", j=BLOCKS)

        def load_w(j0, j1):
            nc.sync.dma_start(out=w_sb[:, j0:j1, :, :], in_=w_view[:, j0:j1, :, :])

        def load_sample(b):
            for n in (0, 2, 1, 3):
                nc.sync.dma_start(
                    out=raw[n * HEAD_PARTS:(n + 1) * HEAD_PARTS, b, :, :],
                    in_=head_res[n, b].rearrange("(q t) d -> q t d", t=PACK),
                )

        def transpose_w(j0, b):
            w_t[j0] = psum.tile([P, 2, 2, P], F32, name="w_t%d" % j0, tag="bank%d" % (SAMPLES + b))
            for j in (0, 1):
                for u in (0, 1):
                    nc.tensor.transpose(w_t[j0][:, j, u, :], w_sb[:, j0 + j, :, :].bitcast(F32)[:, :, u], ident[:])

        def copy_out_w(j0):
            nc.scalar.copy(
                out=w_grouped[:, j0:j0 + 2, :, :].bitcast(F32), in_=w_t[j0][:].rearrange("m j u o -> m j o u")
            )

        def quantise_w(j0, j1):
            nc.vector.quantize_mx(
                out=w_codes[:, j0:j1, :].rearrange("p j o -> p (j o)").bitcast(FP8X4),
                scales=w_scales[:, j0:j1, :].rearrange("p j o -> p (j o)"),
                in_=w_grouped[:, j0:j1, :, :].rearrange("p j o t -> p (j o t)"),
            )

        def regroup(copy, b, d0, d1):
            copy(
                out=grouped[b][:, d0:d1, :].rearrange("p (c i) t -> p c t i", i=4),
                in_=raw[:, b, :, d0:d1].rearrange("p t (c i) -> p c t i", i=4),
            )

        def quantise(b, d0=0, d1=D):
            nc.vector.quantize_mx(
                out=c_codes[:, b, d0:d1].bitcast(FP8X4),
                scales=c_scales[:, b, d0:d1],
                in_=grouped[b][:, d0:d1, :].rearrange("p d t -> p (d t)"),
            )

        def mx_pass(j, b, d0=0, d1=D):
            if d0 == 0:
                acc[(j, b)] = psum.tile([P, D], F32, name="acc%d_%d" % (j, b), tag="bank%d" % (SAMPLES * (j % 2) + b))
            nc.tensor.matmul_mx(
                out=acc[(j, b)][:, d0:d1],
                lhsT=w_codes[:, j, :].bitcast(FP8X4),
                lhsT_scale=w_scales[:, j, :],
                rhs=c_codes[:, b, d0:d1].bitcast(FP8X4),
                rhs_scale=c_scales[:, b, d0:d1],
                start=True,
                stop=True,
            )

        def statistics(j, b):
            nc.vector.bn_stats(out=stats[j][:, b, :], in_=acc[(j, b)][:])

        def aggregate(j):
            nc.vector.bn_aggr(out=mean_var[j][:], in_=stats[j][:].rearrange("p b s -> p (b s)"))

        def negate_gain_mean(j):
            nc.vector.scalar_tensor_tensor(
                out=neg_gain_mean[j][:], in0=mean_var[j][:, 0:1], scalar=-1.0, in1=gain[:, j:j + 1],
                op0=ALU.mult, op1=ALU.mult,
            )

        def inverse_std(j):
            nc.scalar.activation(
                out=inv_std[j][:], in_=mean_var[j][:, 1:2], func=ACT.Abs_reciprocal_sqrt, bias=eps[:, 0:1]
            )

        def scale_shift_on_scalar(j):
            nc.scalar.activation(out=scale[j][:], in_=gain[:, j:j + 1], func=ACT.Copy, scale=inv_std[j][:, 0:1])
            nc.scalar.activation(
                out=shift[j][:], in_=neg_gain_mean[j][:], func=ACT.Identity,
                scale=inv_std[j][:, 0:1], bias=bias[:, j:j + 1],
            )

        def scale_shift_on_vector(j):
            nc.vector.tensor_mul(out=scale[j][:], in0=gain[:, j:j + 1], in1=inv_std[j][:])
            nc.vector.scalar_tensor_tensor(
                out=shift[j][:], in0=neg_gain_mean[j][:], scalar=inv_std[j][:, 0:1], in1=bias[:, j:j + 1],
                op0=ALU.mult, op1=ALU.add,
            )

        def apply_on_scalar(j, b):
            nc.scalar.activation(
                out=result[j][:, b, :], in_=acc[(j, b)][:], func=ACT.Relu,
                scale=scale[j][:, 0:1], bias=shift[j][:, 0:1],
            )

        def affine_on_vector(j, b):
            nc.vector.tensor_scalar(
                out=result[j][:, b, :], in0=acc[(j, b)][:], scalar1=scale[j][:, 0:1], scalar2=shift[j][:, 0:1],
                op0=ALU.mult, op1=ALU.add,
            )

        def relu_on_vector(j, b):
            nc.vector.tensor_scalar_max(out=result[j][:, b, :], in0=result[j][:, b, :], scalar1=0.0)

        def store(j, b):
            nc.sync.dma_start(out=out_view[j][:, b, :], in_=result[j][:, b, :])

        nc.scalar.dma_start(out=gain[:], in_=g_m.rearrange("(p j) -> p j", j=BLOCKS))
        nc.scalar.dma_start(out=bias[:], in_=b_m.rearrange("(p j) -> p j", j=BLOCKS))
        load_sample(0)
        load_w(0, 2)
        for b in (1, 2, 3):
            load_sample(b)
        load_w(2, 4)
        make_identity(nc, ident[:])
        nc.vector.memset(eps[:], EPS)
        nc.scalar.activation(out=warm[:], in_=eps[:], func=ACT.Abs_reciprocal_sqrt)

        transpose_w(0, 0)
        regroup(nc.scalar.copy, 0, V_COLS[0], D)
        copy_out_w(0)
        regroup(nc.scalar.copy, 1, V_COLS[1], D)
        regroup(nc.scalar.copy, 2, V_COLS[2], D)
        regroup(nc.vector.tensor_copy, 0, 0, V_COLS[0])
        quantise(0)
        regroup(nc.vector.tensor_copy, 1, 0, V_COLS[1])
        quantise_w(0, 2)
        mx_pass(0, 0)
        mx_pass(1, 0)
        quantise(1)
        mx_pass(0, 1)
        mx_pass(1, 1)
        statistics(0, 0)
        regroup(nc.vector.tensor_copy, 2, 0, V_COLS[2])
        statistics(1, 0)
        quantise(2)
        mx_pass(0, 2)
        statistics(0, 1)

        regroup(nc.scalar.copy, 3, V_COLS[3], D)
        regroup(nc.vector.tensor_copy, 3, 0, D // 2)
        regroup(nc.vector.tensor_copy, 3, D // 2, V_COLS[3])
        transpose_w(2, 3)
        for d0 in (0, D // 2):
            quantise(3, d0, d0 + D // 2)
            mx_pass(0, 3, d0, d0 + D // 2)
        copy_out_w(2)
        mx_pass(1, 2)
        mx_pass(1, 3)
        statistics(0, 2)
        statistics(0, 3)
        aggregate(0)
        inverse_std(0)
        quantise_w(2, 4)
        negate_gain_mean(0)
        scale_shift_on_scalar(0)
        for b in (1, 2, 3):
            statistics(1, b)
        aggregate(1)

        for j in range(BLOCKS - 1):
            for b in range(SAMPLES - 1):
                apply_on_scalar(j, b)
                store(j, b)
                if j + 2 < BLOCKS:
                    mx_pass(j + 2, b)
            inverse_std(j + 1)
            apply_on_scalar(j, SAMPLES - 1)
            store(j, SAMPLES - 1)
            if j + 2 < BLOCKS:
                mx_pass(j + 2, SAMPLES - 1)
                statistics(j + 2, 0)
            negate_gain_mean(j + 1)
            scale_shift_on_vector(j + 1)
            if j + 2 < BLOCKS:
                for b in range(1, SAMPLES):
                    statistics(j + 2, b)
                aggregate(j + 2)
        affine_on_vector(3, 3)
        relu_on_vector(3, 3)
        for b in (0, 1):
            apply_on_scalar(3, b)
            store(3, b)
        store(3, 3)
        apply_on_scalar(3, 2)
        store(3, 2)
